import numpy as np
import ml_dtypes


def mxq(x, axis, fmt="e4m3"):
    dtype, down = {"e4m3": (ml_dtypes.float8_e4m3fn, 7), "e5m2": (ml_dtypes.float8_e5m2, 14)}[fmt]
    v = np.moveaxis(np.asarray(x, np.float32).astype(ml_dtypes.bfloat16).astype(np.float64), axis, -1)
    blocks = v.reshape(v.shape[:-1] + (-1, 32))
    amax = np.abs(blocks).max(-1, keepdims=True)
    byte = np.maximum(np.where(amax > 0, np.frexp(amax)[1] - 1 + 127, 0) - down, 1)
    scale = np.exp2(byte - 127.0)
    codes = (blocks / scale).astype(np.float32).astype(dtype).astype(np.float64)
    return np.moveaxis((codes * scale).reshape(v.shape), -1, axis)


WIDE = False


def mx_kscale(k):
    if not WIDE:
        return np.ones(k)
    levels = np.array([20, -20, 10, -10, 0])
    a = np.random.permutation(np.resize(levels, k // 512 * 4)).reshape(k // 512, 4)
    idx = np.arange(k)
    return np.exp2(a[idx // 512, idx % 128 // 32])


BF16 = ml_dtypes.bfloat16


def bf(x):
    return np.asarray(x, np.float32).astype(BF16)


def f64(x):
    return np.asarray(x).astype(np.float64)


B, N, D, H, K = 8, 256, 1024, 512, 512
NT = B * N
LN2PI_2 = np.log(2.0 * np.pi) / 2.0


def setup_inputs():
    s = mx_kscale(K)
    cent = 0.4 * np.random.standard_normal((B, D))
    idx = np.random.randint(0, B, K)
    xf = np.repeat(cent, N, axis=0) + 0.5 * np.random.standard_normal((NT, D))
    mean = 0.6 * cent[idx] + 0.1 * np.random.standard_normal((K, D))
    var = 0.35 * np.exp(0.2 * np.random.standard_normal((K, D))) * s[:, None]
    g = np.random.standard_normal((NT, K)) * np.exp2(np.random.randint(-12, 1, (NT, 1))) * s[None, :]
    return {"xf": bf(xf), "mean": bf(mean), "var": bf(var), "grad_out": bf(g)}


def reference(xf, mean, var, grad_out):
    xv, mv, vv = f64(xf), f64(mean), f64(var)
    inv_var = 1.0 / vv
    gq = mxq(f64(grad_out), 1, "e5m2")
    a = gq @ mxq(mv * inv_var, 0, "e4m3")
    b = gq @ mxq(inv_var, 0, "e4m3")
    return a - xv * b

@@ -1,0 +1,274 @@
+from contextlib import ExitStack
+
+import concourse.mybir as mybir
+from concourse.masks import make_identity
+
+F32 = mybir.dt.float32
+BF16 = mybir.dt.bfloat16
+U32 = mybir.dt.uint32
+U8 = mybir.dt.uint8
+E4M3_X4 = mybir.dt.float8_e4m3fn_x4
+E5M2_X4 = mybir.dt.float8_e5m2_x4
+ACT = mybir.ActivationFunctionType
+ALU = mybir.AluOpType
+
+P = 128
+PACK = 4
+NT, D, K = 2048, 1024, 512
+assert K == P * PACK
+
+TILES = NT // P
+HALF = 512
+HALVES = D // HALF
+UNITS = HALVES * TILES
+CHUNK = 256
+CHUNKS = HALF // CHUNK
+GROUP = 4
+GROUPS = TILES // GROUP
+WORDS = K // 2
+
+FLOPS = 2 * 2 * NT * K * D
+
+
+def tile_gaussianmlpbasislayer_pb_kernel(tc, xf, mean, var, grad_out, out):
+    nc = tc.nc
+
+    var_rows = var.rearrange("(p j) d -> p j d", j=PACK)
+    mean_rows = mean.rearrange("(p j) d -> p j d", j=PACK)
+    grad_rows = grad_out.rearrange("(p t) k -> p (t k)", t=TILES)
+    xf_rows = xf.rearrange("(p t) d -> p t d", t=TILES)
+    out_rows = out.rearrange("(p t) d -> p t d", t=TILES)
+
+    with ExitStack() as ctx:
+        keep = ctx.enter_context(tc.tile_pool(name="keep", bufs=1))
+        work = ctx.enter_context(tc.tile_pool(name="work", bufs=2))
+        products = ctx.enter_context(tc.tile_pool(name="products", bufs=3))
+        results = ctx.enter_context(tc.tile_pool(name="results", bufs=4))
+        sums = ctx.enter_context(tc.psum_pool(name="sums", bufs=6))
+        turns = ctx.enter_context(tc.psum_pool(name="turns", bufs=2))
+        ctx.enter_context(tc.manual_schedule())
+
+        var_sb = [keep.tile([P, PACK, HALF], BF16, name="var_sb%d" % h) for h in range(HALVES)]
+        mean_sb = [keep.tile([P, PACK, HALF], BF16, name="mean_sb%d" % h) for h in range(HALVES)]
+        grad_sb = keep.tile([P, TILES * K], BF16)
+        xf_sb = keep.tile([P, TILES, D], BF16)
+
+        inv_bf = [
+            keep.tile([P, HALF * PACK], BF16, name="inv_bf%d" % h, align_bytes=64)
+            for h in range(HALVES)
+        ]
+        ratio_bf = [
+            keep.tile([P, HALF * PACK], BF16, name="ratio_bf%d" % h, align_bytes=64)
+            for h in range(HALVES)
+        ]
+        inv_codes = keep.tile([P, HALVES, HALF], U32, align_bytes=64)
+        inv_scales = keep.tile([P, HALVES, HALF], U8, align_bytes=64)
+        ratio_codes = keep.tile([P, HALVES, HALF], U32, align_bytes=64)
+        ratio_scales = keep.tile([P, HALVES, HALF], U8, align_bytes=64)
+        grad_codes = keep.tile([P, NT], U32, align_bytes=64)
+        grad_scales = keep.tile([P, NT], U8, align_bytes=64)
+
+        def load_half(tiles, rows, h):
+            nc.sync.dma_start(out=tiles[h][:], in_=rows[:, :, h * HALF : (h + 1) * HALF])
+
+        def load_grad(group):
+            cols = slice(group * GROUP * K, (group + 1) * GROUP * K)
+            nc.sync.dma_start(out=grad_sb[:, cols], in_=grad_rows[:, cols])
+
+        def load_xf(group):
+            tiles = slice(group * GROUP, (group + 1) * GROUP)
+            nc.sync.dma_start(out=xf_sb[:, tiles, :], in_=xf_rows[:, tiles, :])
+
+        load_half(var_sb, var_rows, 0)
+        load_grad(0)
+        load_half(mean_sb, mean_rows, 0)
+        load_xf(0)
+        load_grad(1)
+        load_half(var_sb, var_rows, 1)
+        load_half(mean_sb, mean_rows, 1)
+        for group in range(1, GROUPS):
+            if group + 1 < GROUPS:
+                load_grad(group + 1)
+            load_xf(group)
+
+        ident = keep.tile([P, P], F32)
+        make_identity(nc, ident[:])
+
+        one = keep.tile([P, 1], F32)
+        warm = keep.tile([P, 1], F32)
+        nc.vector.memset(one[:], 1.0)
+        nc.scalar.activation(out=warm[:], in_=one[:], func=ACT.Abs_reciprocal_sqrt)
+
+        guess_of, neg_xy_of, inv_of = {}, {}, {}
+
+        def rows_side_by_side(tiles, q):
+            h, c = divmod(q, CHUNKS)
+            return tiles[h][:, :, c * CHUNK : (c + 1) * CHUNK].rearrange("p j w -> p w j")
+
+        def chunk_of(tiles, q):
+            h, c = divmod(q, CHUNKS)
+            flat = tiles[h][:, c * CHUNK * PACK : (c + 1) * CHUNK * PACK]
+            return flat.rearrange("p (w j) -> p w j", j=PACK)
+
+        def seed(q):
+            rsqrt = work.tile([P, CHUNK, PACK], F32)
+            nc.scalar.activation(
+                out=rsqrt[:], in_=rows_side_by_side(var_sb, q), func=ACT.Abs_reciprocal_sqrt
+            )
+            guess = work.tile([P, CHUNK, PACK], F32)
+            nc.scalar.activation(out=guess[:], in_=rsqrt[:], func=ACT.Square)
+            guess_of[q] = guess
+
+        def residual(q):
+            neg_xy = work.tile([P, CHUNK, PACK], F32)
+            nc.vector.scalar_tensor_tensor(
+                out=neg_xy[:],
+                in0=rows_side_by_side(var_sb, q),
+                scalar=-1.0,
+                in1=guess_of[q][:],
+                op0=ALU.mult,
+                op1=ALU.mult,
+            )
+            neg_xy_of[q] = neg_xy
+
+        def refine(q):
+            inv = work.tile([P, CHUNK, PACK], F32)
+            nc.vector.scalar_tensor_tensor(
+                out=inv[:],
+                in0=neg_xy_of[q][:],
+                scalar=2.0,
+                in1=guess_of[q][:],
+                op0=ALU.add,
+                op1=ALU.mult,
+            )
+            inv_of[q] = inv
+
+        def finish(q):
+            nc.scalar.copy(out=chunk_of(inv_bf, q), in_=inv_of[q][:])
+            nc.vector.tensor_tensor(
+                out=chunk_of(ratio_bf, q),
+                in0=rows_side_by_side(mean_sb, q),
+                in1=inv_of[q][:],
+                op=ALU.mult,
+            )
+
+        def quantise_weights(h):
+            nc.vector.quantize_mx(
+                out=inv_codes[:, h, :].bitcast(E4M3_X4), scales=inv_scales[:, h, :], in_=inv_bf[h][:]
+            )
+            nc.vector.quantize_mx(
+                out=ratio_codes[:, h, :].bitcast(E4M3_X4),
+                scales=ratio_scales[:, h, :],
+                in_=ratio_bf[h][:],
+            )
+
+        grad_words = grad_sb[:].bitcast(F32)
+        grouped_of = {}
+
+        def transpose_group(group):
+            grouped = work.tile([P, GROUP * P * PACK], BF16, align_bytes=64)
+            grouped_words = grouped[:].bitcast(F32).rearrange("p (i n u) -> p i n u", n=P, u=2)
+            for pair in range(GROUP // 2):
+                turned = turns.tile([P, 2, 2, P], F32)
+                for i in range(2):
+                    t = group * GROUP + 2 * pair + i
+                    words = grad_words[:, t * WORDS : (t + 1) * WORDS].rearrange(
+                        "p (q u) -> p u q", u=2
+                    )
+                    for u in range(2):
+                        nc.tensor.transpose(turned[:, i, u, :], words[:, u, :], ident[:])
+                nc.scalar.copy(
+                    out=grouped_words[:, 2 * pair : 2 * pair + 2, :, :],
+                    in_=turned[:].rearrange("p i u n -> p i n u"),
+                )
+            grouped_of[group] = grouped
+
+        def quantise_group(group):
+            cols = slice(group * GROUP * P, (group + 1) * GROUP * P)
+            nc.vector.quantize_mx(
+                out=grad_codes[:, cols].bitcast(E5M2_X4),
+                scales=grad_scales[:, cols],
+                in_=grouped_of[group][:],
+            )
+
+        a_of, b_of, xb_of = {}, {}, {}
+
+        def passes(unit):
+            h, t = divmod(unit, TILES)
+            instances = slice(t * P, (t + 1) * P)
+            b_ps = sums.tile([P, HALF], F32, tag="sum")
+            nc.tensor.matmul_mx(
+                out=b_ps[:],
+                lhsT=grad_codes[:, instances].bitcast(E5M2_X4),
+                lhsT_scale=grad_scales[:, instances],
+                rhs=inv_codes[:, h, :].bitcast(E4M3_X4),
+                rhs_scale=inv_scales[:, h, :],
+                start=True,
+                stop=True,
+            )
+            a_ps = sums.tile([P, HALF], F32, tag="sum")
+            nc.tensor.matmul_mx(
+                out=a_ps[:],
+                lhsT=grad_codes[:, instances].bitcast(E5M2_X4),
+                lhsT_scale=grad_scales[:, instances],
+                rhs=ratio_codes[:, h, :].bitcast(E4M3_X4),
+                rhs_scale=ratio_scales[:, h, :],
+                start=True,
+                stop=True,
+            )
+            a_of[unit], b_of[unit] = a_ps, b_ps
+
+        def product(unit):
+            h, t = divmod(unit, TILES)
+            xb = products.tile([P, HALF], F32)
+            nc.vector.tensor_tensor(
+                out=xb[:],
+                in0=b_of[unit][:],
+                in1=xf_sb[:, t, h * HALF : (h + 1) * HALF],
+                op=ALU.mult,
+            )
+            xb_of[unit] = xb
+
+        def difference(unit):
+            h, t = divmod(unit, TILES)
+            res = results.tile([P, HALF], F32)
+            nc.vector.tensor_tensor(out=res[:], in0=a_of[unit][:], in1=xb_of[unit][:], op=ALU.subtract)
+            nc.sync.dma_start(out=out_rows[:, t, h * HALF : (h + 1) * HALF], in_=res[:])
+
+        seed(0)
+        seed(1)
+        transpose_group(0)
+        residual(0)
+        refine(0)
+        residual(1)
+        refine(1)
+        quantise_group(0)
+        finish(0)
+        finish(1)
+        quantise_weights(0)
+
+        stages = (seed, residual, refine, finish)
+
+        def prepare_ahead(t):
+            group, place = divmod(t, GROUP)
+            if group + 1 < GROUPS and place == 0:
+                transpose_group(group + 1)
+            if group + 1 < GROUPS and place == 2:
+                quantise_group(group + 1)
+            step, odd = divmod(t, 2)
+            if odd == 0:
+                for depth in reversed(range(len(stages))):
+                    c = step - depth
+                    if 0 <= c < CHUNKS:
+                        stages[depth](CHUNKS + c)
+                if step == len(stages) + CHUNKS:
+                    quantise_weights(1)
+
+        for unit in range(UNITS + 1):
+            if unit < UNITS:
+                if unit < TILES:
+                    prepare_ahead(unit)
+                passes(unit)
+                product(unit)
+            if unit >= 1:
+                difference(unit - 1)

@@ -44,6 +44,7 @@ def tile_gaussianmlpbasislayer_pb_kernel(tc, xf, mean, var, grad_out, out):
         work = ctx.enter_context(tc.tile_pool(name="work", bufs=2))
         products = ctx.enter_context(tc.tile_pool(name="products", bufs=3))
         results = ctx.enter_context(tc.tile_pool(name="results", bufs=4))
+        copies = ctx.enter_context(tc.tile_pool(name="copies", bufs=3))
         sums = ctx.enter_context(tc.psum_pool(name="sums", bufs=6))
         turns = ctx.enter_context(tc.psum_pool(name="turns", bufs=2))
         ctx.enter_context(tc.manual_schedule())
@@ -229,11 +230,26 @@ def tile_gaussianmlpbasislayer_pb_kernel(tc, xf, mean, var, grad_out, out):
             )
             xb_of[unit] = xb
 
-        def difference(unit):
+        def store(unit, res):
             h, t = divmod(unit, TILES)
+            nc.sync.dma_start(out=out_rows[:, t, h * HALF : (h + 1) * HALF], in_=res[:])
+
+        def difference(unit):
             res = results.tile([P, HALF], F32)
             nc.vector.tensor_tensor(out=res[:], in0=a_of[unit][:], in1=xb_of[unit][:], op=ALU.subtract)
-            nc.sync.dma_start(out=out_rows[:, t, h * HALF : (h + 1) * HALF], in_=res[:])
+            store(unit, res)
+
+        def beside_vector(unit):
+            h, t = divmod(unit, TILES)
+            b_sb = copies.tile([P, HALF], F32)
+            nc.scalar.copy(out=b_sb[:], in_=b_of[unit][:])
+            a_sb = copies.tile([P, HALF], F32)
+            nc.scalar.copy(out=a_sb[:], in_=a_of[unit][:])
+            nc.gpsimd.tensor_tensor(
+                out=b_sb[:], in0=b_sb[:], in1=xf_sb[:, t, h * HALF : (h + 1) * HALF], op=ALU.mult
+            )
+            nc.gpsimd.tensor_tensor(out=a_sb[:], in0=a_sb[:], in1=b_sb[:], op=ALU.subtract)
+            return a_sb
 
         seed(0)
         seed(1)
@@ -264,11 +280,20 @@ def tile_gaussianmlpbasislayer_pb_kernel(tc, xf, mean, var, grad_out, out):
                 if step == len(stages) + CHUNKS:
                     quantise_weights(1)
 
-        for unit in range(UNITS + 1):
-            if unit < UNITS:
-                if unit < TILES:
-                    prepare_ahead(unit)
-                passes(unit)
+        vector_unit = None
+        gpsimd_unit, gpsimd_res = None, None
+        for unit in range(UNITS):
+            if unit < TILES:
+                prepare_ahead(unit)
+            passes(unit)
+            if unit % 5 in (2, 4):
+                if gpsimd_unit is not None:
+                    store(gpsimd_unit, gpsimd_res)
+                gpsimd_unit, gpsimd_res = unit, beside_vector(unit)
+            else:
                 product(unit)
-            if unit >= 1:
-                difference(unit - 1)
+                if vector_unit is not None:
+                    difference(vector_unit)
+                vector_unit = unit
+        difference(vector_unit)
+        store(gpsimd_unit, gpsimd_res)

@@ -20,12 +20,13 @@ assert K == P * PACK
 TILES = NT // P
 HALF = 512
 HALVES = D // HALF
-UNITS = HALVES * TILES
+BANKS = 8
 CHUNK = 256
-CHUNKS = HALF // CHUNK
+CHUNKS = D // CHUNK
 GROUP = 4
 GROUPS = TILES // GROUP
 WORDS = K // 2
+GPSIMD_EVERY = 3
 
 FLOPS = 2 * 2 * NT * K * D
 
@@ -41,56 +42,37 @@ def tile_gaussianmlpbasislayer_pb_kernel(tc, xf, mean, var, grad_out, out):
 
     with ExitStack() as ctx:
         keep = ctx.enter_context(tc.tile_pool(name="keep", bufs=1))
-        work = ctx.enter_context(tc.tile_pool(name="work", bufs=2))
-        products = ctx.enter_context(tc.tile_pool(name="products", bufs=3))
-        results = ctx.enter_context(tc.tile_pool(name="results", bufs=4))
-        copies = ctx.enter_context(tc.tile_pool(name="copies", bufs=3))
-        sums = ctx.enter_context(tc.psum_pool(name="sums", bufs=6))
-        turns = ctx.enter_context(tc.psum_pool(name="turns", bufs=2))
+        work = ctx.enter_context(tc.tile_pool(name="work", bufs=3))
+        stream = ctx.enter_context(tc.tile_pool(name="stream", bufs=2))
+        results = ctx.enter_context(tc.tile_pool(name="results", bufs=3))
+        psum = ctx.enter_context(tc.psum_pool(name="psum", bufs=BANKS))
         ctx.enter_context(tc.manual_schedule())
 
-        var_sb = [keep.tile([P, PACK, HALF], BF16, name="var_sb%d" % h) for h in range(HALVES)]
-        mean_sb = [keep.tile([P, PACK, HALF], BF16, name="mean_sb%d" % h) for h in range(HALVES)]
+        var_sb = keep.tile([P, PACK, D], BF16)
+        mean_sb = keep.tile([P, PACK, D], BF16)
         grad_sb = keep.tile([P, TILES * K], BF16)
         xf_sb = keep.tile([P, TILES, D], BF16)
 
-        inv_bf = [
-            keep.tile([P, HALF * PACK], BF16, name="inv_bf%d" % h, align_bytes=64)
-            for h in range(HALVES)
-        ]
-        ratio_bf = [
-            keep.tile([P, HALF * PACK], BF16, name="ratio_bf%d" % h, align_bytes=64)
-            for h in range(HALVES)
-        ]
-        inv_codes = keep.tile([P, HALVES, HALF], U32, align_bytes=64)
-        inv_scales = keep.tile([P, HALVES, HALF], U8, align_bytes=64)
-        ratio_codes = keep.tile([P, HALVES, HALF], U32, align_bytes=64)
-        ratio_scales = keep.tile([P, HALVES, HALF], U8, align_bytes=64)
+        inv_bf = keep.tile([P, D, PACK], BF16, align_bytes=64)
+        ratio_bf = keep.tile([P, D, PACK], BF16, align_bytes=64)
+        grad_bf = keep.tile([P, NT * PACK], BF16, align_bytes=64)
+        inv_codes = keep.tile([P, D], U32, align_bytes=64)
+        inv_scales = keep.tile([P, D], U8, align_bytes=64)
+        ratio_codes = keep.tile([P, D], U32, align_bytes=64)
+        ratio_scales = keep.tile([P, D], U8, align_bytes=64)
         grad_codes = keep.tile([P, NT], U32, align_bytes=64)
         grad_scales = keep.tile([P, NT], U8, align_bytes=64)
 
-        def load_half(tiles, rows, h):
-            nc.sync.dma_start(out=tiles[h][:], in_=rows[:, :, h * HALF : (h + 1) * HALF])
-
-        def load_grad(group):
+        for tile_sb, rows in ((var_sb, var_rows), (mean_sb, mean_rows)):
+            for h in range(HALVES):
+                cols = slice(h * HALF, (h + 1) * HALF)
+                nc.sync.dma_start(out=tile_sb[:, :, cols], in_=rows[:, :, cols])
+        for group in range(GROUPS):
             cols = slice(group * GROUP * K, (group + 1) * GROUP * K)
             nc.sync.dma_start(out=grad_sb[:, cols], in_=grad_rows[:, cols])
-
-        def load_xf(group):
+        for group in range(GROUPS):
             tiles = slice(group * GROUP, (group + 1) * GROUP)
             nc.sync.dma_start(out=xf_sb[:, tiles, :], in_=xf_rows[:, tiles, :])
-
-        load_half(var_sb, var_rows, 0)
-        load_grad(0)
-        load_half(mean_sb, mean_rows, 0)
-        load_xf(0)
-        load_grad(1)
-        load_half(var_sb, var_rows, 1)
-        load_half(mean_sb, mean_rows, 1)
-        for group in range(1, GROUPS):
-            if group + 1 < GROUPS:
-                load_grad(group + 1)
-            load_xf(group)
 
         ident = keep.tile([P, P], F32)
         make_identity(nc, ident[:])
@@ -102,198 +84,152 @@ def tile_gaussianmlpbasislayer_pb_kernel(tc, xf, mean, var, grad_out, out):
 
         guess_of, neg_xy_of, inv_of = {}, {}, {}
 
-        def rows_side_by_side(tiles, q):
-            h, c = divmod(q, CHUNKS)
-            return tiles[h][:, :, c * CHUNK : (c + 1) * CHUNK].rearrange("p j w -> p w j")
+        def rows_side_by_side(tile_sb, c):
+            return tile_sb[:, :, c * CHUNK : (c + 1) * CHUNK].rearrange("p j w -> p w j")
 
-        def chunk_of(tiles, q):
-            h, c = divmod(q, CHUNKS)
-            flat = tiles[h][:, c * CHUNK * PACK : (c + 1) * CHUNK * PACK]
-            return flat.rearrange("p (w j) -> p w j", j=PACK)
-
-        def seed(q):
+        def seed(c):
             rsqrt = work.tile([P, CHUNK, PACK], F32)
             nc.scalar.activation(
-                out=rsqrt[:], in_=rows_side_by_side(var_sb, q), func=ACT.Abs_reciprocal_sqrt
+                out=rsqrt[:], in_=rows_side_by_side(var_sb, c), func=ACT.Abs_reciprocal_sqrt
             )
             guess = work.tile([P, CHUNK, PACK], F32)
             nc.scalar.activation(out=guess[:], in_=rsqrt[:], func=ACT.Square)
-            guess_of[q] = guess
+            guess_of[c] = guess
 
-        def residual(q):
+        def residual(c):
             neg_xy = work.tile([P, CHUNK, PACK], F32)
             nc.vector.scalar_tensor_tensor(
                 out=neg_xy[:],
-                in0=rows_side_by_side(var_sb, q),
+                in0=rows_side_by_side(var_sb, c),
                 scalar=-1.0,
-                in1=guess_of[q][:],
+                in1=guess_of[c][:],
                 op0=ALU.mult,
                 op1=ALU.mult,
             )
-            neg_xy_of[q] = neg_xy
+            neg_xy_of[c] = neg_xy
 
-        def refine(q):
+        def refine(c):
             inv = work.tile([P, CHUNK, PACK], F32)
             nc.vector.scalar_tensor_tensor(
                 out=inv[:],
-                in0=neg_xy_of[q][:],
+                in0=neg_xy_of[c][:],
                 scalar=2.0,
-                in1=guess_of[q][:],
+                in1=guess_of[c][:],
                 op0=ALU.add,
                 op1=ALU.mult,
             )
-            inv_of[q] = inv
+            inv_of[c] = inv
 
-        def finish(q):
-            nc.scalar.copy(out=chunk_of(inv_bf, q), in_=inv_of[q][:])
+        def round_inv(c):
+            nc.scalar.copy(out=inv_bf[:, c * CHUNK : (c + 1) * CHUNK, :], in_=inv_of[c][:])
+
+        def round_ratio(c):
             nc.vector.tensor_tensor(
-                out=chunk_of(ratio_bf, q),
-                in0=rows_side_by_side(mean_sb, q),
-                in1=inv_of[q][:],
+                out=ratio_bf[:, c * CHUNK : (c + 1) * CHUNK, :],
+                in0=rows_side_by_side(mean_sb, c),
+                in1=inv_of[c][:],
                 op=ALU.mult,
             )
 
-        def quantise_weights(h):
-            nc.vector.quantize_mx(
-                out=inv_codes[:, h, :].bitcast(E4M3_X4), scales=inv_scales[:, h, :], in_=inv_bf[h][:]
-            )
-            nc.vector.quantize_mx(
-                out=ratio_codes[:, h, :].bitcast(E4M3_X4),
-                scales=ratio_scales[:, h, :],
-                in_=ratio_bf[h][:],
-            )
+        for step in range(CHUNKS + 2):
+            if step < CHUNKS:
+                seed(step)
+            if 1 <= step <= CHUNKS:
+                residual(step - 1)
+            if 2 <= step:
+                round_ratio(step - 2)
+                round_inv(step - 2)
+            if 1 <= step <= CHUNKS:
+                refine(step - 1)
 
         grad_words = grad_sb[:].bitcast(F32)
-        grouped_of = {}
+        grad_bf_words = grad_bf[:].bitcast(F32).rearrange("p (t n u) -> p t n u", n=P, u=2)
+        for pair in range(TILES // 2):
+            turned = psum.tile([P, 2, 2, P], F32, tag="bank")
+            for i in range(2):
+                t = 2 * pair + i
+                words = grad_words[:, t * WORDS : (t + 1) * WORDS].rearrange("p (q u) -> p u q", u=2)
+                for u in range(2):
+                    nc.tensor.transpose(turned[:, i, u, :], words[:, u, :], ident[:])
+            nc.scalar.copy(
+                out=grad_bf_words[:, 2 * pair : 2 * pair + 2, :, :],
+                in_=turned[:].rearrange("p i u n -> p i n u"),
+            )
 
-        def transpose_group(group):
-            grouped = work.tile([P, GROUP * P * PACK], BF16, align_bytes=64)
-            grouped_words = grouped[:].bitcast(F32).rearrange("p (i n u) -> p i n u", n=P, u=2)
-            for pair in range(GROUP // 2):
-                turned = turns.tile([P, 2, 2, P], F32)
-                for i in range(2):
-                    t = group * GROUP + 2 * pair + i
-                    words = grad_words[:, t * WORDS : (t + 1) * WORDS].rearrange(
-                        "p (q u) -> p u q", u=2
-                    )
-                    for u in range(2):
-                        nc.tensor.transpose(turned[:, i, u, :], words[:, u, :], ident[:])
-                nc.scalar.copy(
-                    out=grouped_words[:, 2 * pair : 2 * pair + 2, :, :],
-                    in_=turned[:].rearrange("p i u n -> p i n u"),
-                )
-            grouped_of[group] = grouped
-
-        def quantise_group(group):
+        for h in range(HALVES):
+            cols = slice(h * HALF, (h + 1) * HALF)
+            nc.vector.quantize_mx(
+                out=inv_codes[:, cols].bitcast(E4M3_X4),
+                scales=inv_scales[:, cols],
+                in_=inv_bf[:, cols, :].rearrange("p w j -> p (w j)"),
+            )
+            nc.vector.quantize_mx(
+                out=ratio_codes[:, cols].bitcast(E4M3_X4),
+                scales=ratio_scales[:, cols],
+                in_=ratio_bf[:, cols, :].rearrange("p w j -> p (w j)"),
+            )
+        for group in range(GROUPS):
             cols = slice(group * GROUP * P, (group + 1) * GROUP * P)
             nc.vector.quantize_mx(
                 out=grad_codes[:, cols].bitcast(E5M2_X4),
                 scales=grad_scales[:, cols],
-                in_=grouped_of[group][:],
+                in_=grad_bf[:, group * GROUP * P * PACK : (group + 1) * GROUP * P * PACK],
             )
 
-        a_of, b_of, xb_of = {}, {}, {}
-
-        def passes(unit):
-            h, t = divmod(unit, TILES)
+        def passes(t, codes, scales):
             instances = slice(t * P, (t + 1) * P)
-            b_ps = sums.tile([P, HALF], F32, tag="sum")
-            nc.tensor.matmul_mx(
-                out=b_ps[:],
-                lhsT=grad_codes[:, instances].bitcast(E5M2_X4),
-                lhsT_scale=grad_scales[:, instances],
-                rhs=inv_codes[:, h, :].bitcast(E4M3_X4),
-                rhs_scale=inv_scales[:, h, :],
-                start=True,
-                stop=True,
-            )
-            a_ps = sums.tile([P, HALF], F32, tag="sum")
-            nc.tensor.matmul_mx(
-                out=a_ps[:],
-                lhsT=grad_codes[:, instances].bitcast(E5M2_X4),
-                lhsT_scale=grad_scales[:, instances],
-                rhs=ratio_codes[:, h, :].bitcast(E4M3_X4),
-                rhs_scale=ratio_scales[:, h, :],
-                start=True,
-                stop=True,
-            )
-            a_of[unit], b_of[unit] = a_ps, b_ps
+            banks = []
+            for h in range(HALVES):
+                cols = slice(h * HALF, (h + 1) * HALF)
+                bank = psum.tile([P, HALF], F32, name="bank%d" % h, tag="bank")
+                nc.tensor.matmul_mx(
+                    out=bank[:],
+                    lhsT=grad_codes[:, instances].bitcast(E5M2_X4),
+                    lhsT_scale=grad_scales[:, instances],
+                    rhs=codes[:, cols].bitcast(E4M3_X4),
+                    rhs_scale=scales[:, cols],
+                    start=True,
+                    stop=True,
+                )
+                banks.append(bank)
+            return banks
 
-        def product(unit):
-            h, t = divmod(unit, TILES)
-            xb = products.tile([P, HALF], F32)
-            nc.vector.tensor_tensor(
-                out=xb[:],
-                in0=b_of[unit][:],
-                in1=xf_sb[:, t, h * HALF : (h + 1) * HALF],
-                op=ALU.mult,
-            )
-            xb_of[unit] = xb
+        def store(t, res):
+            nc.sync.dma_start(out=out_rows[:, t, :], in_=res[:])
 
-        def store(unit, res):
-            h, t = divmod(unit, TILES)
-            nc.sync.dma_start(out=out_rows[:, t, h * HALF : (h + 1) * HALF], in_=res[:])
+        def on_vector(t, a_banks, b_banks):
+            xb = stream.tile([P, D], F32)
+            res = results.tile([P, D], F32)
+            for h in range(HALVES):
+                cols = slice(h * HALF, (h + 1) * HALF)
+                nc.vector.tensor_tensor(
+                    out=xb[:, cols], in0=b_banks[h][:], in1=xf_sb[:, t, cols], op=ALU.mult
+                )
+            for h in range(HALVES):
+                cols = slice(h * HALF, (h + 1) * HALF)
+                nc.vector.tensor_tensor(
+                    out=res[:, cols], in0=a_banks[h][:], in1=xb[:, cols], op=ALU.subtract
+                )
+            return res
 
-        def difference(unit):
-            res = results.tile([P, HALF], F32)
-            nc.vector.tensor_tensor(out=res[:], in0=a_of[unit][:], in1=xb_of[unit][:], op=ALU.subtract)
-            store(unit, res)
-
-        def beside_vector(unit):
-            h, t = divmod(unit, TILES)
-            b_sb = copies.tile([P, HALF], F32)
-            nc.scalar.copy(out=b_sb[:], in_=b_of[unit][:])
-            a_sb = copies.tile([P, HALF], F32)
-            nc.scalar.copy(out=a_sb[:], in_=a_of[unit][:])
-            nc.gpsimd.tensor_tensor(
-                out=b_sb[:], in0=b_sb[:], in1=xf_sb[:, t, h * HALF : (h + 1) * HALF], op=ALU.mult
-            )
+        def on_gpsimd(t, a_banks, b_banks):
+            b_sb = stream.tile([P, D], F32)
+            a_sb = stream.tile([P, D], F32)
+            for tile_sb, banks in ((b_sb, b_banks), (a_sb, a_banks)):
+                for h in range(HALVES):
+                    nc.scalar.copy(out=tile_sb[:, h * HALF : (h + 1) * HALF], in_=banks[h][:])
+            nc.gpsimd.tensor_tensor(out=b_sb[:], in0=b_sb[:], in1=xf_sb[:, t, :], op=ALU.mult)
             nc.gpsimd.tensor_tensor(out=a_sb[:], in0=a_sb[:], in1=b_sb[:], op=ALU.subtract)
             return a_sb
 
-        seed(0)
-        seed(1)
-        transpose_group(0)
-        residual(0)
-        refine(0)
-        residual(1)
-        refine(1)
-        quantise_group(0)
-        finish(0)
-        finish(1)
-        quantise_weights(0)
-
-        stages = (seed, residual, refine, finish)
-
-        def prepare_ahead(t):
-            group, place = divmod(t, GROUP)
-            if group + 1 < GROUPS and place == 0:
-                transpose_group(group + 1)
-            if group + 1 < GROUPS and place == 2:
-                quantise_group(group + 1)
-            step, odd = divmod(t, 2)
-            if odd == 0:
-                for depth in reversed(range(len(stages))):
-                    c = step - depth
-                    if 0 <= c < CHUNKS:
-                        stages[depth](CHUNKS + c)
-                if step == len(stages) + CHUNKS:
-                    quantise_weights(1)
-
-        vector_unit = None
-        gpsimd_unit, gpsimd_res = None, None
-        for unit in range(UNITS):
-            if unit < TILES:
-                prepare_ahead(unit)
-            passes(unit)
-            if unit % 5 in (2, 4):
-                if gpsimd_unit is not None:
-                    store(gpsimd_unit, gpsimd_res)
-                gpsimd_unit, gpsimd_res = unit, beside_vector(unit)
+        late_t, late_res = None, None
+        for t in range(TILES):
+            b_banks = passes(t, inv_codes, inv_scales)
+            a_banks = passes(t, ratio_codes, ratio_scales)
+            if t % GPSIMD_EVERY == 0 and t != TILES - 1:
+                if late_t is not None:
+                    store(late_t, late_res)
+                late_t, late_res = t, on_gpsimd(t, a_banks, b_banks)
             else:
-                product(unit)
-                if vector_unit is not None:
-                    difference(vector_unit)
-                vector_unit = unit
-        difference(vector_unit)
-        store(gpsimd_unit, gpsimd_res)
+                store(t, on_vector(t, a_banks, b_banks))
+        store(late_t, late_res)

@@ -63,10 +63,12 @@ def tile_gaussianmlpbasislayer_pb_kernel(tc, xf, mean, var, grad_out, out):
         grad_codes = keep.tile([P, NT], U32, align_bytes=64)
         grad_scales = keep.tile([P, NT], U8, align_bytes=64)
 
-        for tile_sb, rows in ((var_sb, var_rows), (mean_sb, mean_rows)):
-            for h in range(HALVES):
-                cols = slice(h * HALF, (h + 1) * HALF)
-                nc.sync.dma_start(out=tile_sb[:, :, cols], in_=rows[:, :, cols])
+        for c in range(CHUNKS):
+            cols = slice(c * CHUNK, (c + 1) * CHUNK)
+            nc.sync.dma_start(out=var_sb[:, :, cols], in_=var_rows[:, :, cols])
+        for h in range(HALVES):
+            cols = slice(h * HALF, (h + 1) * HALF)
+            nc.sync.dma_start(out=mean_sb[:, :, cols], in_=mean_rows[:, :, cols])
         for group in range(GROUPS):
             cols = slice(group * GROUP * K, (group + 1) * GROUP * K)
             nc.sync.dma_start(out=grad_sb[:, cols], in_=grad_rows[:, cols])
@@ -76,11 +78,6 @@ def tile_gaussianmlpbasislayer_pb_kernel(tc, xf, mean, var, grad_out, out):
 
         ident = keep.tile([P, P], F32)
         make_identity(nc, ident[:])
-
-        one = keep.tile([P, 1], F32)
-        warm = keep.tile([P, 1], F32)
-        nc.vector.memset(one[:], 1.0)
-        nc.scalar.activation(out=warm[:], in_=one[:], func=ACT.Abs_reciprocal_sqrt)
 
         guess_of, neg_xy_of, inv_of = {}, {}, {}
 
@@ -131,20 +128,10 @@ def tile_gaussianmlpbasislayer_pb_kernel(tc, xf, mean, var, grad_out, out):
                 op=ALU.mult,
             )
 
-        for step in range(CHUNKS + 2):
-            if step < CHUNKS:
-                seed(step)
-            if 1 <= step <= CHUNKS:
-                residual(step - 1)
-            if 2 <= step:
-                round_ratio(step - 2)
-                round_inv(step - 2)
-            if 1 <= step <= CHUNKS:
-                refine(step - 1)
-
         grad_words = grad_sb[:].bitcast(F32)
         grad_bf_words = grad_bf[:].bitcast(F32).rearrange("p (t n u) -> p t n u", n=P, u=2)
-        for pair in range(TILES // 2):
+
+        def turn(pair):
             turned = psum.tile([P, 2, 2, P], F32, tag="bank")
             for i in range(2):
                 t = 2 * pair + i
@@ -156,25 +143,43 @@ def tile_gaussianmlpbasislayer_pb_kernel(tc, xf, mean, var, grad_out, out):
                 in_=turned[:].rearrange("p i u n -> p i n u"),
             )
 
-        for h in range(HALVES):
+        for step in range(CHUNKS + 2):
+            if step < CHUNKS:
+                seed(step)
+            if 1 <= step <= CHUNKS:
+                residual(step - 1)
+            if 2 <= step:
+                round_ratio(step - 2)
+                round_inv(step - 2)
+            if 1 <= step <= CHUNKS:
+                refine(step - 1)
+            if step >= CHUNKS:
+                for pair in range((step - CHUNKS) * TILES // 4, (step - CHUNKS + 1) * TILES // 4):
+                    turn(pair)
+
+        def quantise_weights(weights_bf, codes, scales, h):
             cols = slice(h * HALF, (h + 1) * HALF)
             nc.vector.quantize_mx(
-                out=inv_codes[:, cols].bitcast(E4M3_X4),
-                scales=inv_scales[:, cols],
-                in_=inv_bf[:, cols, :].rearrange("p w j -> p (w j)"),
+                out=codes[:, cols].bitcast(E4M3_X4),
+                scales=scales[:, cols],
+                in_=weights_bf[:, cols, :].rearrange("p w j -> p (w j)"),
             )
-            nc.vector.quantize_mx(
-                out=ratio_codes[:, cols].bitcast(E4M3_X4),
-                scales=ratio_scales[:, cols],
-                in_=ratio_bf[:, cols, :].rearrange("p w j -> p (w j)"),
-            )
-        for group in range(GROUPS):
+
+        def quantise_grad(group):
             cols = slice(group * GROUP * P, (group + 1) * GROUP * P)
             nc.vector.quantize_mx(
                 out=grad_codes[:, cols].bitcast(E5M2_X4),
                 scales=grad_scales[:, cols],
                 in_=grad_bf[:, group * GROUP * P * PACK : (group + 1) * GROUP * P * PACK],
             )
+
+        quantise_weights(inv_bf, inv_codes, inv_scales, 0)
+        quantise_grad(0)
+        quantise_weights(inv_bf, inv_codes, inv_scales, 1)
+        quantise_weights(ratio_bf, ratio_codes, ratio_scales, 0)
+        quantise_weights(ratio_bf, ratio_codes, ratio_scales, 1)
+        for group in range(1, GROUPS):
+            quantise_grad(group)
 
         def passes(t, codes, scales):
             instances = slice(t * P, (t + 1) * P)
@@ -195,7 +200,9 @@ def tile_gaussianmlpbasislayer_pb_kernel(tc, xf, mean, var, grad_out, out):
             return banks
 
         def store(t, res):
-            nc.sync.dma_start(out=out_rows[:, t, :], in_=res[:])
+            for h in range(HALVES):
+                cols = slice(h * HALF, (h + 1) * HALF)
+                nc.sync.dma_start(out=out_rows[:, t, cols], in_=res[:, cols])
 
         def on_vector(t, a_banks, b_banks):
             xb = stream.tile([P, D], F32)
@@ -219,7 +226,11 @@ def tile_gaussianmlpbasislayer_pb_kernel(tc, xf, mean, var, grad_out, out):
                 for h in range(HALVES):
                     nc.scalar.copy(out=tile_sb[:, h * HALF : (h + 1) * HALF], in_=banks[h][:])
             nc.gpsimd.tensor_tensor(out=b_sb[:], in0=b_sb[:], in1=xf_sb[:, t, :], op=ALU.mult)
-            nc.gpsimd.tensor_tensor(out=a_sb[:], in0=a_sb[:], in1=b_sb[:], op=ALU.subtract)
+            for h in range(HALVES):
+                cols = slice(h * HALF, (h + 1) * HALF)
+                nc.gpsimd.tensor_tensor(
+                    out=a_sb[:, cols], in0=a_sb[:, cols], in1=b_sb[:, cols], op=ALU.subtract
+                )
             return a_sb
 
         late_t, late_res = None, None

from contextlib import ExitStack

import concourse.mybir as mybir
from concourse.masks import make_identity

F32 = mybir.dt.float32
BF16 = mybir.dt.bfloat16
U32 = mybir.dt.uint32
U8 = mybir.dt.uint8
E4M3_X4 = mybir.dt.float8_e4m3fn_x4
E5M2_X4 = mybir.dt.float8_e5m2_x4
ACT = mybir.ActivationFunctionType
ALU = mybir.AluOpType

P = 128
PACK = 4
NT, D, K = 2048, 1024, 512
assert K == P * PACK

TILES = NT // P
HALF = 512
HALVES = D // HALF
BANKS = 8
CHUNK = 256
CHUNKS = D // CHUNK
GROUP = 4
GROUPS = TILES // GROUP
WORDS = K // 2
GPSIMD_EVERY = 3

FLOPS = 2 * 2 * NT * K * D


def tile_gaussianmlpbasislayer_pb_kernel(tc, xf, mean, var, grad_out, out):
    nc = tc.nc

    var_rows = var.rearrange("(p j) d -> p j d", j=PACK)
    mean_rows = mean.rearrange("(p j) d -> p j d", j=PACK)
    grad_rows = grad_out.rearrange("(p t) k -> p (t k)", t=TILES)
    xf_rows = xf.rearrange("(p t) d -> p t d", t=TILES)
    out_rows = out.rearrange("(p t) d -> p t d", t=TILES)

    with ExitStack() as ctx:
        keep = ctx.enter_context(tc.tile_pool(name="keep", bufs=1))
        work = ctx.enter_context(tc.tile_pool(name="work", bufs=3))
        stream = ctx.enter_context(tc.tile_pool(name="stream", bufs=2))
        results = ctx.enter_context(tc.tile_pool(name="results", bufs=3))
        psum = ctx.enter_context(tc.psum_pool(name="psum", bufs=BANKS))
        ctx.enter_context(tc.manual_schedule())

        var_sb = keep.tile([P, PACK, D], BF16)
        mean_sb = keep.tile([P, PACK, D], BF16)
        grad_sb = keep.tile([P, TILES * K], BF16)
        xf_sb = keep.tile([P, TILES, D], BF16)

        inv_bf = keep.tile([P, D, PACK], BF16, align_bytes=64)
        ratio_bf = keep.tile([P, D, PACK], BF16, align_bytes=64)
        grad_bf = keep.tile([P, NT * PACK], BF16, align_bytes=64)
        inv_codes = keep.tile([P, D], U32, align_bytes=64)
        inv_scales = keep.tile([P, D], U8, align_bytes=64)
        ratio_codes = keep.tile([P, D], U32, align_bytes=64)
        ratio_scales = keep.tile([P, D], U8, align_bytes=64)
        grad_codes = keep.tile([P, NT], U32, align_bytes=64)
        grad_scales = keep.tile([P, NT], U8, align_bytes=64)

        for c in range(CHUNKS):
            cols = slice(c * CHUNK, (c + 1) * CHUNK)
            nc.sync.dma_start(out=var_sb[:, :, cols], in_=var_rows[:, :, cols])
        for h in range(HALVES):
            cols = slice(h * HALF, (h + 1) * HALF)
            nc.sync.dma_start(out=mean_sb[:, :, cols], in_=mean_rows[:, :, cols])
        for group in range(GROUPS):
            cols = slice(group * GROUP * K, (group + 1) * GROUP * K)
            nc.sync.dma_start(out=grad_sb[:, cols], in_=grad_rows[:, cols])
        for group in range(GROUPS):
            tiles = slice(group * GROUP, (group + 1) * GROUP)
            nc.sync.dma_start(out=xf_sb[:, tiles, :], in_=xf_rows[:, tiles, :])

        ident = keep.tile([P, P], F32)
        make_identity(nc, ident[:])

        guess_of, neg_xy_of, inv_of = {}, {}, {}

        def rows_side_by_side(tile_sb, c):
            return tile_sb[:, :, c * CHUNK : (c + 1) * CHUNK].rearrange("p j w -> p w j")

        def seed(c):
            rsqrt = work.tile([P, CHUNK, PACK], F32)
            nc.scalar.activation(
                out=rsqrt[:], in_=rows_side_by_side(var_sb, c), func=ACT.Abs_reciprocal_sqrt
            )
            guess = work.tile([P, CHUNK, PACK], F32)
            nc.scalar.activation(out=guess[:], in_=rsqrt[:], func=ACT.Square)
            guess_of[c] = guess

        def residual(c):
            neg_xy = work.tile([P, CHUNK, PACK], F32)
            nc.vector.scalar_tensor_tensor(
                out=neg_xy[:],
                in0=rows_side_by_side(var_sb, c),
                scalar=-1.0,
                in1=guess_of[c][:],
                op0=ALU.mult,
                op1=ALU.mult,
            )
            neg_xy_of[c] = neg_xy

        def refine(c):
            inv = work.tile([P, CHUNK, PACK], F32)
            nc.vector.scalar_tensor_tensor(
                out=inv[:],
                in0=neg_xy_of[c][:],
                scalar=2.0,
                in1=guess_of[c][:],
                op0=ALU.add,
                op1=ALU.mult,
            )
            inv_of[c] = inv

        def round_inv(c):
            nc.scalar.copy(out=inv_bf[:, c * CHUNK : (c + 1) * CHUNK, :], in_=inv_of[c][:])

        def round_ratio(c):
            nc.vector.tensor_tensor(
                out=ratio_bf[:, c * CHUNK : (c + 1) * CHUNK, :],
                in0=rows_side_by_side(mean_sb, c),
                in1=inv_of[c][:],
                op=ALU.mult,
            )

        grad_words = grad_sb[:].bitcast(F32)
        grad_bf_words = grad_bf[:].bitcast(F32).rearrange("p (t n u) -> p t n u", n=P, u=2)

        def turn(pair):
            turned = psum.tile([P, 2, 2, P], F32, tag="bank")
            for i in range(2):
                t = 2 * pair + i
                words = grad_words[:, t * WORDS : (t + 1) * WORDS].rearrange("p (q u) -> p u q", u=2)
                for u in range(2):
                    nc.tensor.transpose(turned[:, i, u, :], words[:, u, :], ident[:])
            nc.scalar.copy(
                out=grad_bf_words[:, 2 * pair : 2 * pair + 2, :, :],
                in_=turned[:].rearrange("p i u n -> p i n u"),
            )

        for step in range(CHUNKS + 2):
            if step < CHUNKS:
                seed(step)
            if 1 <= step <= CHUNKS:
                residual(step - 1)
            if 2 <= step:
                round_ratio(step - 2)
                round_inv(step - 2)
            if 1 <= step <= CHUNKS:
                refine(step - 1)
            if step >= CHUNKS:
                for pair in range((step - CHUNKS) * TILES // 4, (step - CHUNKS + 1) * TILES // 4):
                    turn(pair)

        def quantise_weights(weights_bf, codes, scales, h):
            cols = slice(h * HALF, (h + 1) * HALF)
            nc.vector.quantize_mx(
                out=codes[:, cols].bitcast(E4M3_X4),
                scales=scales[:, cols],
                in_=weights_bf[:, cols, :].rearrange("p w j -> p (w j)"),
            )

        def quantise_grad(group):
            cols = slice(group * GROUP * P, (group + 1) * GROUP * P)
            nc.vector.quantize_mx(
                out=grad_codes[:, cols].bitcast(E5M2_X4),
                scales=grad_scales[:, cols],
                in_=grad_bf[:, group * GROUP * P * PACK : (group + 1) * GROUP * P * PACK],
            )

        quantise_weights(inv_bf, inv_codes, inv_scales, 0)
        quantise_grad(0)
        quantise_weights(inv_bf, inv_codes, inv_scales, 1)
        quantise_weights(ratio_bf, ratio_codes, ratio_scales, 0)
        quantise_weights(ratio_bf, ratio_codes, ratio_scales, 1)
        for group in range(1, GROUPS):
            quantise_grad(group)

        def passes(t, codes, scales):
            instances = slice(t * P, (t + 1) * P)
            banks = []
            for h in range(HALVES):
                cols = slice(h * HALF, (h + 1) * HALF)
                bank = psum.tile([P, HALF], F32, name="bank%d" % h, tag="bank")
                nc.tensor.matmul_mx(
                    out=bank[:],
                    lhsT=grad_codes[:, instances].bitcast(E5M2_X4),
                    lhsT_scale=grad_scales[:, instances],
                    rhs=codes[:, cols].bitcast(E4M3_X4),
                    rhs_scale=scales[:, cols],
                    start=True,
                    stop=True,
                )
                banks.append(bank)
            return banks

        def store(t, res):
            for h in range(HALVES):
                cols = slice(h * HALF, (h + 1) * HALF)
                nc.sync.dma_start(out=out_rows[:, t, cols], in_=res[:, cols])

        def on_vector(t, a_banks, b_banks):
            xb = stream.tile([P, D], F32)
            res = results.tile([P, D], F32)
            for h in range(HALVES):
                cols = slice(h * HALF, (h + 1) * HALF)
                nc.vector.tensor_tensor(
                    out=xb[:, cols], in0=b_banks[h][:], in1=xf_sb[:, t, cols], op=ALU.mult
                )
            for h in range(HALVES):
                cols = slice(h * HALF, (h + 1) * HALF)
                nc.vector.tensor_tensor(
                    out=res[:, cols], in0=a_banks[h][:], in1=xb[:, cols], op=ALU.subtract
                )
            return res

        def on_gpsimd(t, a_banks, b_banks):
            b_sb = stream.tile([P, D], F32)
            a_sb = stream.tile([P, D], F32)
            for tile_sb, banks in ((b_sb, b_banks), (a_sb, a_banks)):
                for h in range(HALVES):
                    nc.scalar.copy(out=tile_sb[:, h * HALF : (h + 1) * HALF], in_=banks[h][:])
            nc.gpsimd.tensor_tensor(out=b_sb[:], in0=b_sb[:], in1=xf_sb[:, t, :], op=ALU.mult)
            for h in range(HALVES):
                cols = slice(h * HALF, (h + 1) * HALF)
                nc.gpsimd.tensor_tensor(
                    out=a_sb[:, cols], in0=a_sb[:, cols], in1=b_sb[:, cols], op=ALU.subtract
                )
            return a_sb

        late_t, late_res = None, None
        for t in range(TILES):
            b_banks = passes(t, inv_codes, inv_scales)
            a_banks = passes(t, ratio_codes, ratio_scales)
            if t % GPSIMD_EVERY == 0 and t != TILES - 1:
                if late_t is not None:
                    store(late_t, late_res)
                late_t, late_res = t, on_gpsimd(t, a_banks, b_banks)
            else:
                store(t, on_vector(t, a_banks, b_banks))
        store(late_t, late_res)
